import numpy as np
import ml_dtypes


def mxq(x, axis, fmt="e4m3"):
    dtype, down = {"e4m3": (ml_dtypes.float8_e4m3fn, 7), "e5m2": (ml_dtypes.float8_e5m2, 14)}[fmt]
    v = np.moveaxis(np.asarray(x, np.float32).astype(ml_dtypes.bfloat16).astype(np.float64), axis, -1)
    blocks = v.reshape(v.shape[:-1] + (-1, 32))
    amax = np.abs(blocks).max(-1, keepdims=True)
    byte = np.maximum(np.where(amax > 0, np.frexp(amax)[1] - 1 + 127, 0) - down, 1)
    scale = np.exp2(byte - 127.0)
    codes = (blocks / scale).astype(np.float32).astype(dtype).astype(np.float64)
    return np.moveaxis((codes * scale).reshape(v.shape), -1, axis)


WIDE = False


def mx_kscale(k):
    if not WIDE:
        return np.ones(k)
    levels = np.array([10, -10, 5, -5, 0])
    a = np.random.permutation(np.resize(levels, k // 512 * 4)).reshape(k // 512, 4)
    idx = np.arange(k)
    return np.exp2(a[idx // 512, idx % 128 // 32])


BF16 = ml_dtypes.bfloat16


def bf(x):
    return np.asarray(x, np.float32).astype(BF16)


def f64(x):
    return np.asarray(x).astype(np.float64)


T, B, D, H, HD, A = 512, 1, 1024, 16, 128, 128
HH = H * HD
CAT = HH + D
EPS = 1e-5
AO = 0.6


def layer_norm(x, w, b):
    mu = x.mean(-1, keepdims=True)
    var = np.square(x - mu).mean(-1, keepdims=True)
    return (x - mu) * (1.0 / np.sqrt(var + EPS)) * w + b


def setup_inputs():
    t = mx_kscale(HH)
    w_out = np.random.standard_normal((CAT, D)) / np.sqrt(CAT)
    w_out[:HH] = w_out[:HH] / t[:, None]
    return {"u": bf(np.random.standard_normal((T, B, HH)) * t),
            "attn_out": bf(AO * np.random.standard_normal((T, B, HH)) * t),
            "src_norm": bf(np.random.standard_normal((T, B, D))),
            "w_out": bf(w_out),
            "b_out": bf(0.1 * np.random.standard_normal(D)),
            "ln2_w": bf(1.0 + 0.1 * np.random.standard_normal(D)),
            "ln2_b": bf(0.1 * np.random.standard_normal(D))}


def reference(u, attn_out, src_norm, w_out, b_out, ln2_w, ln2_b):
    residual = f64(u) + f64(attn_out)
    xn = f64(src_norm)
    cat = np.concatenate([residual, xn], -1)
    z = (mxq(cat, 2, "e4m3") @ mxq(f64(w_out), 0, "e4m3")) + f64(b_out)
    return layer_norm(z, f64(ln2_w), f64(ln2_b)) + xn

@@ -1,0 +1,231 @@
+from contextlib import ExitStack
+
+import concourse.mybir as mybir
+from concourse.masks import make_identity
+
+F32 = mybir.dt.float32
+BF16 = mybir.dt.bfloat16
+U32 = mybir.dt.uint32
+U8 = mybir.dt.uint8
+FP8X4 = mybir.dt.float8_e4m3fn_x4
+ALU = mybir.AluOpType
+ACT = mybir.ActivationFunctionType
+
+P = 128
+PACK = 4
+K_PASS = P * PACK
+TOKENS = 512
+RES = 2048
+D = 1024
+K = RES + D
+BANK = 512
+EPS = 1e-5
+
+TOKEN_TILES = TOKENS // P
+PASSES = K // K_PASS
+RES_PASSES = RES // K_PASS
+SRC_PASSES = D // K_PASS
+HALVES = D // BANK
+WORDS = K_PASS // 2
+
+FLOPS = 2 * TOKENS * K * D
+
+
+def transpose_words(nc, psum, rows, passes, grouped, ident_f32):
+    words = rows.bitcast(F32)
+    grouped_words = grouped.bitcast(F32).rearrange("p (g t h) -> p g t h", t=P, h=2)
+    for pair in range(passes // 2):
+        flipped = psum.tile([P, 4, P], F32, tag="bank")
+        for q in range(4):
+            first = (pair * 4 + q) * P
+            nc.tensor.transpose(flipped[:, q, :], words[:, first : first + P], ident_f32)
+        nc.scalar.copy(
+            out=grouped_words[:, 2 * pair : 2 * pair + 2, :, :],
+            in_=flipped[:].rearrange("p (g h) t -> p g t h", h=2),
+        )
+
+
+def tile_stulayer_pb_kernel(tc, u, attn_out, src_norm, w_out, b_out, ln2_w, ln2_b, out):
+    nc = tc.nc
+    u_rows = u.rearrange("t b f -> (t b) f")
+    attn_rows = attn_out.rearrange("t b f -> (t b) f")
+    src_rows = src_norm.rearrange("t b f -> (t b) f")
+    out_rows = out.rearrange("t b f -> (t b) f")
+
+    with ExitStack() as ctx:
+        keep = ctx.enter_context(tc.tile_pool(name="keep", bufs=1))
+        loads = ctx.enter_context(tc.tile_pool(name="loads", bufs=4))
+        stage = ctx.enter_context(tc.tile_pool(name="stage", bufs=2))
+        wraw = ctx.enter_context(tc.tile_pool(name="wraw", bufs=PASSES))
+        psum = ctx.enter_context(tc.psum_pool(name="psum", bufs=8))
+
+        eps = keep.tile([P, 1], F32)
+        nc.vector.memset(eps[:], EPS)
+        warm = keep.tile([P, 1], F32)
+        nc.scalar.activation(out=warm[:], in_=eps[:], func=ACT.Sqrt)
+
+        ident_f32 = keep.tile([P, P], F32)
+        make_identity(nc, ident_f32[:])
+        ident_bf16 = keep.tile([P, P], BF16)
+        make_identity(nc, ident_bf16[:])
+        ones = keep.tile([P, P], BF16)
+        nc.vector.memset(ones[:], 1.0)
+
+        vec_rows = keep.tile([P, P], BF16)
+        nc.vector.memset(vec_rows[:], 0.0)
+        nc.scalar.dma_start(out=vec_rows[0:8, :], in_=b_out.rearrange("(r c) -> r c", c=P))
+        nc.scalar.dma_start(out=vec_rows[8:16, :], in_=ln2_w.rearrange("(r c) -> r c", c=P))
+        shift_row = keep.tile([P, D], BF16)
+        nc.vector.memset(shift_row[:], 0.0)
+        nc.scalar.dma_start(out=shift_row[0:1, :], in_=ln2_b.rearrange("(o c) -> o c", o=1))
+
+        vec_cols_ps = psum.tile([P, P], BF16, tag="bank")
+        nc.tensor.transpose(vec_cols_ps[:], vec_rows[:], ident_bf16[:])
+        vec_cols = keep.tile([P, P], BF16)
+        nc.vector.tensor_copy(out=vec_cols[:], in_=vec_cols_ps[:])
+        bias_all = keep.tile([P, D], BF16)
+        gain_all = keep.tile([P, D], BF16)
+        for first_row, spread in ((0, bias_all), (8, gain_all)):
+            spread_ps = psum.tile([P, D], BF16, tag="bank")
+            for r in range(D // P):
+                column = vec_cols[:, first_row + r : first_row + r + 1]
+                nc.tensor.transpose(
+                    spread_ps[:, r * P : (r + 1) * P], column.to_broadcast([P, P]), ident_bf16[:]
+                )
+            nc.vector.tensor_copy(out=spread[:], in_=spread_ps[:])
+
+        cat_codes = keep.tile([P, TOKEN_TILES, PASSES * P], U32, align_bytes=64)
+        cat_scales = keep.tile([P, TOKEN_TILES, PASSES * P], U8, align_bytes=64)
+        src_tiles = []
+        for i in range(TOKEN_TILES):
+            rows = slice(i * P, (i + 1) * P)
+            u_t = loads.tile([P, RES], BF16)
+            nc.sync.dma_start(out=u_t[:], in_=u_rows[rows, :])
+            attn_t = loads.tile([P, RES], BF16)
+            nc.sync.dma_start(out=attn_t[:], in_=attn_rows[rows, :])
+            src_t = keep.tile([P, D], BF16, name="src%d" % i)
+            nc.sync.dma_start(out=src_t[:], in_=src_rows[rows, :])
+            src_tiles.append(src_t)
+
+            residual = stage.tile([P, RES], BF16)
+            nc.vector.tensor_tensor(out=residual[:], in0=u_t[:], in1=attn_t[:], op=ALU.add)
+
+            res_grouped = stage.tile([P, RES_PASSES * K_PASS], BF16, align_bytes=64)
+            transpose_words(nc, psum, residual[:], RES_PASSES, res_grouped[:], ident_f32[:])
+            src_grouped = stage.tile([P, SRC_PASSES * K_PASS], BF16, align_bytes=64)
+            transpose_words(nc, psum, src_t[:], SRC_PASSES, src_grouped[:], ident_f32[:])
+
+            split = RES_PASSES * P
+            nc.vector.quantize_mx(
+                out=cat_codes[:, i, 0:split].bitcast(FP8X4),
+                scales=cat_scales[:, i, 0:split],
+                in_=res_grouped[:],
+            )
+            nc.vector.quantize_mx(
+                out=cat_codes[:, i, split:].bitcast(FP8X4),
+                scales=cat_scales[:, i, split:],
+                in_=src_grouped[:],
+            )
+
+        w_codes = keep.tile([P, PASSES, D], U32, align_bytes=64)
+        w_scales = keep.tile([P, PASSES, D], U8, align_bytes=64)
+        acc = [
+            [psum.tile([P, BANK], F32, tag="bank", name="acc%d%d" % (i, h)) for h in range(HALVES)]
+            for i in range(TOKEN_TILES)
+        ]
+        for g in range(PASSES):
+            raw = wraw.tile([P, PACK, D], BF16)
+            nc.sync.dma_start(
+                out=raw[:].rearrange("p (h e) c -> p h e c", e=2),
+                in_=w_out[g * K_PASS : (g + 1) * K_PASS, :].rearrange("(h p e) c -> p h e c", h=2, e=2),
+            )
+            grouped = stage.tile([P, D * PACK], BF16, align_bytes=64)
+            for h in range(HALVES):
+                copy = nc.vector.tensor_copy if h == 0 else nc.scalar.copy
+                copy(
+                    out=grouped[:, h * BANK * PACK : (h + 1) * BANK * PACK].rearrange(
+                        "p (c i t) -> p c t i", i=4, t=PACK
+                    ),
+                    in_=raw[:, :, h * BANK : (h + 1) * BANK].rearrange("p t (c i) -> p c t i", i=4),
+                )
+            for h in range(HALVES):
+                cols = slice(h * BANK, (h + 1) * BANK)
+                nc.vector.quantize_mx(
+                    out=w_codes[:, g, cols].bitcast(FP8X4),
+                    scales=w_scales[:, g, cols],
+                    in_=grouped[:, h * BANK * PACK : (h + 1) * BANK * PACK],
+                )
+            for i in range(TOKEN_TILES):
+                for h in range(HALVES):
+                    cols = slice(h * BANK, (h + 1) * BANK)
+                    nc.tensor.matmul_mx(
+                        out=acc[i][h][:],
+                        lhsT=cat_codes[:, i, g * P : (g + 1) * P].bitcast(FP8X4),
+                        lhsT_scale=cat_scales[:, i, g * P : (g + 1) * P],
+                        rhs=w_codes[:, g, cols].bitcast(FP8X4),
+                        rhs_scale=w_scales[:, g, cols],
+                        start=(g == 0),
+                        stop=(g == PASSES - 1),
+                    )
+
+        for i in range(TOKEN_TILES):
+            z = stage.tile([P, D], F32)
+            z_sum = stage.tile([P, HALVES], F32)
+            for h in range(HALVES):
+                cols = slice(h * BANK, (h + 1) * BANK)
+                nc.vector.scalar_tensor_tensor(
+                    out=z[:, cols],
+                    in0=acc[i][h][:],
+                    scalar=1.0,
+                    in1=bias_all[:, cols],
+                    op0=ALU.mult,
+                    op1=ALU.add,
+                    accum_out=z_sum[:, h : h + 1],
+                )
+            neg_mean = stage.tile([P, 1], F32)
+            nc.vector.tensor_scalar(
+                out=neg_mean[:],
+                in0=z_sum[:, 0:1],
+                scalar1=z_sum[:, 1:2],
+                scalar2=-1.0 / D,
+                op0=ALU.add,
+                op1=ALU.mult,
+            )
+            shifted = []
+            for h in range(HALVES):
+                cols = slice(h * BANK, (h + 1) * BANK)
+                shifted_ps = psum.tile([P, BANK], F32, tag="bank", name="shifted%d" % h)
+                nc.tensor.matmul(
+                    out=shifted_ps[:], lhsT=ident_bf16[:], rhs=src_tiles[i][:, cols], start=True, stop=False
+                )
+                nc.tensor.matmul(
+                    out=shifted_ps[:], lhsT=ones[:], rhs=shift_row[:, cols], start=False, stop=True
+                )
+                shifted.append(shifted_ps)
+
+            squares = stage.tile([P, D], BF16)
+            sq_sum = stage.tile([P, 1], F32)
+            nc.scalar.activation(
+                out=squares[:], in_=z[:], func=ACT.Square, bias=neg_mean[:], accum_out=sq_sum[:]
+            )
+            std = stage.tile([P, 1], F32)
+            nc.scalar.activation(out=std[:], in_=sq_sum[:], func=ACT.Sqrt, bias=eps[:], scale=1.0 / D)
+            rstd = stage.tile([P, 1], F32)
+            nc.vector.reciprocal(out=rstd[:], in_=std[:])
+
+            gained = stage.tile([P, D], F32)
+            nc.vector.scalar_tensor_tensor(
+                out=gained[:], in0=z[:], scalar=neg_mean[:], in1=gain_all[:], op0=ALU.add, op1=ALU.mult
+            )
+            result = stage.tile([P, D], F32)
+            for h in range(HALVES):
+                cols = slice(h * BANK, (h + 1) * BANK)
+                nc.vector.scalar_tensor_tensor(
+                    out=result[:, cols],
+                    in0=gained[:, cols],
+                    scalar=rstd[:],
+                    in1=shifted[h][:],
+                    op0=ALU.mult,
+                    op1=ALU.add,
+                )
+            nc.sync.dma_start(out=out_rows[i * P : (i + 1) * P, :], in_=result[:])

@@ -22,27 +22,14 @@ BANK = 512
 EPS = 1e-5
 
 TOKEN_TILES = TOKENS // P
+EARLY_TILES = 2
 PASSES = K // K_PASS
 RES_PASSES = RES // K_PASS
-SRC_PASSES = D // K_PASS
 HALVES = D // BANK
-WORDS = K_PASS // 2
+LAG = 2
+PASS_ORDER = list(range(RES_PASSES, PASSES)) + list(range(RES_PASSES))
 
 FLOPS = 2 * TOKENS * K * D
-
-
-def transpose_words(nc, psum, rows, passes, grouped, ident_f32):
-    words = rows.bitcast(F32)
-    grouped_words = grouped.bitcast(F32).rearrange("p (g t h) -> p g t h", t=P, h=2)
-    for pair in range(passes // 2):
-        flipped = psum.tile([P, 4, P], F32, tag="bank")
-        for q in range(4):
-            first = (pair * 4 + q) * P
-            nc.tensor.transpose(flipped[:, q, :], words[:, first : first + P], ident_f32)
-        nc.scalar.copy(
-            out=grouped_words[:, 2 * pair : 2 * pair + 2, :, :],
-            in_=flipped[:].rearrange("p (g h) t -> p g t h", h=2),
-        )
 
 
 def tile_stulayer_pb_kernel(tc, u, attn_out, src_norm, w_out, b_out, ln2_w, ln2_b, out):
@@ -54,22 +41,9 @@ def tile_stulayer_pb_kernel(tc, u, attn_out, src_norm, w_out, b_out, ln2_w, ln2_
 
     with ExitStack() as ctx:
         keep = ctx.enter_context(tc.tile_pool(name="keep", bufs=1))
-        loads = ctx.enter_context(tc.tile_pool(name="loads", bufs=4))
         stage = ctx.enter_context(tc.tile_pool(name="stage", bufs=2))
-        wraw = ctx.enter_context(tc.tile_pool(name="wraw", bufs=PASSES))
+        small = ctx.enter_context(tc.tile_pool(name="small", bufs=TOKEN_TILES))
         psum = ctx.enter_context(tc.psum_pool(name="psum", bufs=8))
-
-        eps = keep.tile([P, 1], F32)
-        nc.vector.memset(eps[:], EPS)
-        warm = keep.tile([P, 1], F32)
-        nc.scalar.activation(out=warm[:], in_=eps[:], func=ACT.Sqrt)
-
-        ident_f32 = keep.tile([P, P], F32)
-        make_identity(nc, ident_f32[:])
-        ident_bf16 = keep.tile([P, P], BF16)
-        make_identity(nc, ident_bf16[:])
-        ones = keep.tile([P, P], BF16)
-        nc.vector.memset(ones[:], 1.0)
 
         vec_rows = keep.tile([P, P], BF16)
         nc.vector.memset(vec_rows[:], 0.0)
@@ -79,10 +53,45 @@ def tile_stulayer_pb_kernel(tc, u, attn_out, src_norm, w_out, b_out, ln2_w, ln2_
         nc.vector.memset(shift_row[:], 0.0)
         nc.scalar.dma_start(out=shift_row[0:1, :], in_=ln2_b.rearrange("(o c) -> o c", o=1))
 
+        u_tiles = [keep.tile([P, RES], BF16, name="u%d" % i) for i in range(TOKEN_TILES)]
+        attn_tiles = [keep.tile([P, RES], BF16, name="attn%d" % i) for i in range(TOKEN_TILES)]
+        src_tiles = [keep.tile([P, D], BF16, name="src%d" % i) for i in range(TOKEN_TILES)]
+        w_raw = [keep.tile([P, PACK, D], BF16, name="w_raw%d" % g) for g in range(PASSES)]
+
+        def load_tokens(i):
+            rows = slice(i * P, (i + 1) * P)
+            nc.sync.dma_start(out=src_tiles[i][:], in_=src_rows[rows, :])
+            nc.sync.dma_start(out=u_tiles[i][:], in_=u_rows[rows, :])
+            nc.sync.dma_start(out=attn_tiles[i][:], in_=attn_rows[rows, :])
+
+        def load_weights(g):
+            nc.sync.dma_start(
+                out=w_raw[g][:].rearrange("p (h e) c -> p h e c", e=2),
+                in_=w_out[g * K_PASS : (g + 1) * K_PASS, :].rearrange("(h p e) c -> p h e c", h=2, e=2),
+            )
+
+        for n, g in enumerate(PASS_ORDER):
+            load_weights(g)
+            if n < EARLY_TILES:
+                load_tokens(n)
+        for i in range(EARLY_TILES, TOKEN_TILES):
+            load_tokens(i)
+
+        eps = keep.tile([P, 1], F32)
+        nc.vector.memset(eps[:], EPS)
+        warm = keep.tile([P, 1], F32)
+        nc.scalar.activation(out=warm[:], in_=eps[:], func=ACT.Sqrt)
+        ident_bf16 = keep.tile([P, P], BF16)
+        make_identity(nc, ident_bf16[:])
+        ident_f32 = keep.tile([P, P], F32)
+        make_identity(nc, ident_f32[:])
+        ones = keep.tile([P, P], BF16)
+        nc.vector.memset(ones[:], 1.0)
+
         vec_cols_ps = psum.tile([P, P], BF16, tag="bank")
         nc.tensor.transpose(vec_cols_ps[:], vec_rows[:], ident_bf16[:])
         vec_cols = keep.tile([P, P], BF16)
-        nc.vector.tensor_copy(out=vec_cols[:], in_=vec_cols_ps[:])
+        nc.scalar.copy(out=vec_cols[:], in_=vec_cols_ps[:])
         bias_all = keep.tile([P, D], BF16)
         gain_all = keep.tile([P, D], BF16)
         for first_row, spread in ((0, bias_all), (8, gain_all)):
@@ -92,97 +101,103 @@ def tile_stulayer_pb_kernel(tc, u, attn_out, src_norm, w_out, b_out, ln2_w, ln2_
                 nc.tensor.transpose(
                     spread_ps[:, r * P : (r + 1) * P], column.to_broadcast([P, P]), ident_bf16[:]
                 )
-            nc.vector.tensor_copy(out=spread[:], in_=spread_ps[:])
+            nc.scalar.copy(out=spread[:], in_=spread_ps[:])
 
         cat_codes = keep.tile([P, TOKEN_TILES, PASSES * P], U32, align_bytes=64)
         cat_scales = keep.tile([P, TOKEN_TILES, PASSES * P], U8, align_bytes=64)
-        src_tiles = []
-        for i in range(TOKEN_TILES):
-            rows = slice(i * P, (i + 1) * P)
-            u_t = loads.tile([P, RES], BF16)
-            nc.sync.dma_start(out=u_t[:], in_=u_rows[rows, :])
-            attn_t = loads.tile([P, RES], BF16)
-            nc.sync.dma_start(out=attn_t[:], in_=attn_rows[rows, :])
-            src_t = keep.tile([P, D], BF16, name="src%d" % i)
-            nc.sync.dma_start(out=src_t[:], in_=src_rows[rows, :])
-            src_tiles.append(src_t)
-
-            residual = stage.tile([P, RES], BF16)
-            nc.vector.tensor_tensor(out=residual[:], in0=u_t[:], in1=attn_t[:], op=ALU.add)
-
-            res_grouped = stage.tile([P, RES_PASSES * K_PASS], BF16, align_bytes=64)
-            transpose_words(nc, psum, residual[:], RES_PASSES, res_grouped[:], ident_f32[:])
-            src_grouped = stage.tile([P, SRC_PASSES * K_PASS], BF16, align_bytes=64)
-            transpose_words(nc, psum, src_t[:], SRC_PASSES, src_grouped[:], ident_f32[:])
-
-            split = RES_PASSES * P
-            nc.vector.quantize_mx(
-                out=cat_codes[:, i, 0:split].bitcast(FP8X4),
-                scales=cat_scales[:, i, 0:split],
-                in_=res_grouped[:],
-            )
-            nc.vector.quantize_mx(
-                out=cat_codes[:, i, split:].bitcast(FP8X4),
-                scales=cat_scales[:, i, split:],
-                in_=src_grouped[:],
-            )
-
         w_codes = keep.tile([P, PASSES, D], U32, align_bytes=64)
         w_scales = keep.tile([P, PASSES, D], U8, align_bytes=64)
-        acc = [
-            [psum.tile([P, BANK], F32, tag="bank", name="acc%d%d" % (i, h)) for h in range(HALVES)]
-            for i in range(TOKEN_TILES)
-        ]
-        for g in range(PASSES):
-            raw = wraw.tile([P, PACK, D], BF16)
-            nc.sync.dma_start(
-                out=raw[:].rearrange("p (h e) c -> p h e c", e=2),
-                in_=w_out[g * K_PASS : (g + 1) * K_PASS, :].rearrange("(h p e) c -> p h e c", h=2, e=2),
+
+        ready_tiles = []
+        ready_weights = []
+        accs = {}
+        issued = {}
+
+        def multiply(i, g, h):
+            cols = slice(h * BANK, (h + 1) * BANK)
+            nc.tensor.matmul_mx(
+                out=accs[i][h][:],
+                lhsT=cat_codes[:, i, g * P : (g + 1) * P].bitcast(FP8X4),
+                lhsT_scale=cat_scales[:, i, g * P : (g + 1) * P],
+                rhs=w_codes[:, g, cols].bitcast(FP8X4),
+                rhs_scale=w_scales[:, g, cols],
+                start=(issued[(i, h)] == 0),
+                stop=(issued[(i, h)] == PASSES - 1),
             )
-            grouped = stage.tile([P, D * PACK], BF16, align_bytes=64)
+            issued[(i, h)] = issued[(i, h)] + 1
+
+        def flip_two_passes(rows):
+            words = rows.bitcast(F32)
+            flipped = psum.tile([P, 4, P], F32, tag="bank")
+            for q in range(4):
+                nc.tensor.transpose(flipped[:, q, :], words[:, q * P : (q + 1) * P], ident_f32[:])
+            grouped = stage.tile([P, 2 * K_PASS], BF16, align_bytes=64, name="cat_grouped", bufs=6)
+            nc.scalar.copy(
+                out=grouped[:].bitcast(F32).rearrange("p (g t h) -> p g t h", t=P, h=2),
+                in_=flipped[:].rearrange("p (g h) t -> p g t h", h=2),
+            )
+            return grouped
+
+        def flip_tokens(i):
+            flips = [(RES_PASSES, flip_two_passes(src_tiles[i][:]))]
+            for first_pass in range(0, RES_PASSES, 2):
+                cols = slice(first_pass * K_PASS, (first_pass + 2) * K_PASS)
+                residual = stage.tile([P, 2 * K_PASS], BF16, bufs=4)
+                nc.vector.tensor_tensor(
+                    out=residual[:], in0=u_tiles[i][:, cols], in1=attn_tiles[i][:, cols], op=ALU.add
+                )
+                flips.append((first_pass, flip_two_passes(residual[:])))
+            return flips
+
+        def quantise_tokens(i, flips):
+            for first_pass, grouped in flips:
+                cols = slice(first_pass * P, (first_pass + 2) * P)
+                nc.vector.quantize_mx(
+                    out=cat_codes[:, i, cols].bitcast(FP8X4), scales=cat_scales[:, i, cols], in_=grouped[:]
+                )
+            accs[i] = [psum.tile([P, BANK], F32, tag="bank", name="acc%d%d" % (i, h)) for h in range(HALVES)]
             for h in range(HALVES):
+                issued[(i, h)] = 0
+            for g, h in ready_weights:
+                multiply(i, g, h)
+            ready_tiles.append(i)
+
+        def regroup_weights(g):
+            halves = []
+            for h in range(HALVES):
+                grouped = stage.tile([P, BANK * PACK], BF16, align_bytes=64, name="w_grouped%d" % h)
                 copy = nc.vector.tensor_copy if h == 0 else nc.scalar.copy
                 copy(
-                    out=grouped[:, h * BANK * PACK : (h + 1) * BANK * PACK].rearrange(
-                        "p (c i t) -> p c t i", i=4, t=PACK
-                    ),
-                    in_=raw[:, :, h * BANK : (h + 1) * BANK].rearrange("p t (c i) -> p c t i", i=4),
+                    out=grouped[:].rearrange("p (c i t) -> p c t i", i=4, t=PACK),
+                    in_=w_raw[g][:, :, h * BANK : (h + 1) * BANK].rearrange("p t (c i) -> p c t i", i=4),
                 )
-            for h in range(HALVES):
-                cols = slice(h * BANK, (h + 1) * BANK)
-                nc.vector.quantize_mx(
-                    out=w_codes[:, g, cols].bitcast(FP8X4),
-                    scales=w_scales[:, g, cols],
-                    in_=grouped[:, h * BANK * PACK : (h + 1) * BANK * PACK],
-                )
-            for i in range(TOKEN_TILES):
-                for h in range(HALVES):
-                    cols = slice(h * BANK, (h + 1) * BANK)
-                    nc.tensor.matmul_mx(
-                        out=acc[i][h][:],
-                        lhsT=cat_codes[:, i, g * P : (g + 1) * P].bitcast(FP8X4),
-                        lhsT_scale=cat_scales[:, i, g * P : (g + 1) * P],
-                        rhs=w_codes[:, g, cols].bitcast(FP8X4),
-                        rhs_scale=w_scales[:, g, cols],
-                        start=(g == 0),
-                        stop=(g == PASSES - 1),
-                    )
+                halves.append(grouped)
+            return halves
 
-        for i in range(TOKEN_TILES):
+        def quantise_weights(g, h, grouped):
+            cols = slice(h * BANK, (h + 1) * BANK)
+            nc.vector.quantize_mx(
+                out=w_codes[:, g, cols].bitcast(FP8X4), scales=w_scales[:, g, cols], in_=grouped[:]
+            )
+            for i in ready_tiles:
+                multiply(i, g, h)
+            ready_weights.append((g, h))
+
+        def centre_and_gain(i):
             z = stage.tile([P, D], F32)
-            z_sum = stage.tile([P, HALVES], F32)
+            z_sum = small.tile([P, HALVES], F32)
             for h in range(HALVES):
                 cols = slice(h * BANK, (h + 1) * BANK)
                 nc.vector.scalar_tensor_tensor(
                     out=z[:, cols],
-                    in0=acc[i][h][:],
+                    in0=accs[i][h][:],
                     scalar=1.0,
                     in1=bias_all[:, cols],
                     op0=ALU.mult,
                     op1=ALU.add,
                     accum_out=z_sum[:, h : h + 1],
                 )
-            neg_mean = stage.tile([P, 1], F32)
+            neg_mean = small.tile([P, 1], F32)
             nc.vector.tensor_scalar(
                 out=neg_mean[:],
                 in0=z_sum[:, 0:1],
@@ -203,20 +218,28 @@ def tile_stulayer_pb_kernel(tc, u, attn_out, src_norm, w_out, b_out, ln2_w, ln2_
                 )
                 shifted.append(shifted_ps)
 
+            gained = stage.tile([P, D], F32, bufs=LAG + 1)
+            if i < TOKEN_TILES - 1:
+                centred = stage.tile([P, D], F32)
+                nc.scalar.activation(out=centred[:], in_=z[:], func=ACT.Identity, bias=neg_mean[:])
+                nc.gpsimd.tensor_tensor(out=gained[:], in0=centred[:], in1=gain_all[:], op=ALU.mult)
+            else:
+                nc.vector.scalar_tensor_tensor(
+                    out=gained[:], in0=z[:], scalar=neg_mean[:], in1=gain_all[:], op0=ALU.add, op1=ALU.mult
+                )
+
             squares = stage.tile([P, D], BF16)
-            sq_sum = stage.tile([P, 1], F32)
+            sq_sum = small.tile([P, 1], F32)
             nc.scalar.activation(
                 out=squares[:], in_=z[:], func=ACT.Square, bias=neg_mean[:], accum_out=sq_sum[:]
             )
-            std = stage.tile([P, 1], F32)
+            std = small.tile([P, 1], F32)
             nc.scalar.activation(out=std[:], in_=sq_sum[:], func=ACT.Sqrt, bias=eps[:], scale=1.0 / D)
-            rstd = stage.tile([P, 1], F32)
-            nc.vector.reciprocal(out=rstd[:], in_=std[:])
+            return gained, std, shifted
 
-            gained = stage.tile([P, D], F32)
-            nc.vector.scalar_tensor_tensor(
-                out=gained[:], in0=z[:], scalar=neg_mean[:], in1=gain_all[:], op0=ALU.add, op1=ALU.mult
-            )
+        def scale_and_store(i, gained, std, shifted):
+            rstd = small.tile([P, 1], F32)
+            nc.vector.reciprocal(out=rstd[:], in_=std[:])
             result = stage.tile([P, D], F32)
             for h in range(HALVES):
                 cols = slice(h * BANK, (h + 1) * BANK)
@@ -228,4 +251,31 @@ def tile_stulayer_pb_kernel(tc, u, attn_out, src_norm, w_out, b_out, ln2_w, ln2_
                     op0=ALU.mult,
                     op1=ALU.add,
                 )
-            nc.sync.dma_start(out=out_rows[i * P : (i + 1) * P, :], in_=result[:])
+                nc.sync.dma_start(out=out_rows[i * P : (i + 1) * P, cols], in_=result[:, cols])
+
+        flips = {}
+        waiting = None
+        for n, g in enumerate(PASS_ORDER):
+            halves = regroup_weights(g)
+            if waiting is not None:
+                quantise_weights(waiting[0], 1, waiting[1])
+            quantise_weights(g, 0, halves[0])
+            waiting = (g, halves[1])
+            if 0 <= n - 1 < EARLY_TILES:
+                quantise_tokens(n - 1, flips[n - 1])
+            if n < EARLY_TILES:
+                flips[n] = flip_tokens(n)
+        quantise_weights(waiting[0], 1, waiting[1])
+
+        ends = {}
+        for i in range(TOKEN_TILES):
+            late = i + EARLY_TILES
+            if late < TOKEN_TILES:
+                flips[late] = flip_tokens(late)
+            if EARLY_TILES <= late - 1 < TOKEN_TILES:
+                quantise_tokens(late - 1, flips[late - 1])
+            if i >= LAG:
+                scale_and_store(i - LAG, *ends[i - LAG])
+            ends[i] = centre_and_gain(i)
+        for i in range(TOKEN_TILES - LAG, TOKEN_TILES):
+            scale_and_store(i, *ends[i])

@@ -80,7 +80,7 @@ def tile_stulayer_pb_kernel(tc, u, attn_out, src_norm, w_out, b_out, ln2_w, ln2_
         eps = keep.tile([P, 1], F32)
         nc.vector.memset(eps[:], EPS)
         warm = keep.tile([P, 1], F32)
-        nc.scalar.activation(out=warm[:], in_=eps[:], func=ACT.Sqrt)
+        nc.scalar.activation(out=warm[:], in_=eps[:], func=ACT.Abs_reciprocal_sqrt)
         ident_bf16 = keep.tile([P, P], BF16)
         make_identity(nc, ident_bf16[:])
         ident_f32 = keep.tile([P, P], F32)
@@ -233,13 +233,13 @@ def tile_stulayer_pb_kernel(tc, u, attn_out, src_norm, w_out, b_out, ln2_w, ln2_
             nc.scalar.activation(
                 out=squares[:], in_=z[:], func=ACT.Square, bias=neg_mean[:], accum_out=sq_sum[:]
             )
-            std = small.tile([P, 1], F32)
-            nc.scalar.activation(out=std[:], in_=sq_sum[:], func=ACT.Sqrt, bias=eps[:], scale=1.0 / D)
-            return gained, std, shifted
-
-        def scale_and_store(i, gained, std, shifted):
             rstd = small.tile([P, 1], F32)
-            nc.vector.reciprocal(out=rstd[:], in_=std[:])
+            nc.scalar.activation(
+                out=rstd[:], in_=sq_sum[:], func=ACT.Abs_reciprocal_sqrt, bias=eps[:], scale=1.0 / D
+            )
+            return gained, rstd, shifted
+
+        def scale_and_store(i, gained, rstd, shifted):
             result = stage.tile([P, D], F32)
             for h in range(HALVES):
                 cols = slice(h * BANK, (h + 1) * BANK)

@@ -219,14 +219,9 @@ def tile_stulayer_pb_kernel(tc, u, attn_out, src_norm, w_out, b_out, ln2_w, ln2_
                 shifted.append(shifted_ps)
 
             gained = stage.tile([P, D], F32, bufs=LAG + 1)
-            if i < TOKEN_TILES - 1:
-                centred = stage.tile([P, D], F32)
-                nc.scalar.activation(out=centred[:], in_=z[:], func=ACT.Identity, bias=neg_mean[:])
-                nc.gpsimd.tensor_tensor(out=gained[:], in0=centred[:], in1=gain_all[:], op=ALU.mult)
-            else:
-                nc.vector.scalar_tensor_tensor(
-                    out=gained[:], in0=z[:], scalar=neg_mean[:], in1=gain_all[:], op0=ALU.add, op1=ALU.mult
-                )
+            nc.vector.scalar_tensor_tensor(
+                out=gained[:], in0=z[:], scalar=neg_mean[:], in1=gain_all[:], op0=ALU.add, op1=ALU.mult
+            )
 
             squares = stage.tile([P, D], BF16)
             sq_sum = small.tile([P, 1], F32)

from contextlib import ExitStack

import concourse.mybir as mybir
from concourse.masks import make_identity

F32 = mybir.dt.float32
BF16 = mybir.dt.bfloat16
U32 = mybir.dt.uint32
U8 = mybir.dt.uint8
FP8X4 = mybir.dt.float8_e4m3fn_x4
ALU = mybir.AluOpType
ACT = mybir.ActivationFunctionType

P = 128
PACK = 4
K_PASS = P * PACK
TOKENS = 512
RES = 2048
D = 1024
K = RES + D
BANK = 512
EPS = 1e-5

TOKEN_TILES = TOKENS // P
EARLY_TILES = 2
PASSES = K // K_PASS
RES_PASSES = RES // K_PASS
HALVES = D // BANK
LAG = 2
PASS_ORDER = list(range(RES_PASSES, PASSES)) + list(range(RES_PASSES))

FLOPS = 2 * TOKENS * K * D


def tile_stulayer_pb_kernel(tc, u, attn_out, src_norm, w_out, b_out, ln2_w, ln2_b, out):
    nc = tc.nc
    u_rows = u.rearrange("t b f -> (t b) f")
    attn_rows = attn_out.rearrange("t b f -> (t b) f")
    src_rows = src_norm.rearrange("t b f -> (t b) f")
    out_rows = out.rearrange("t b f -> (t b) f")

    with ExitStack() as ctx:
        keep = ctx.enter_context(tc.tile_pool(name="keep", bufs=1))
        stage = ctx.enter_context(tc.tile_pool(name="stage", bufs=2))
        small = ctx.enter_context(tc.tile_pool(name="small", bufs=TOKEN_TILES))
        psum = ctx.enter_context(tc.psum_pool(name="psum", bufs=8))

        vec_rows = keep.tile([P, P], BF16)
        nc.vector.memset(vec_rows[:], 0.0)
        nc.scalar.dma_start(out=vec_rows[0:8, :], in_=b_out.rearrange("(r c) -> r c", c=P))
        nc.scalar.dma_start(out=vec_rows[8:16, :], in_=ln2_w.rearrange("(r c) -> r c", c=P))
        shift_row = keep.tile([P, D], BF16)
        nc.vector.memset(shift_row[:], 0.0)
        nc.scalar.dma_start(out=shift_row[0:1, :], in_=ln2_b.rearrange("(o c) -> o c", o=1))

        u_tiles = [keep.tile([P, RES], BF16, name="u%d" % i) for i in range(TOKEN_TILES)]
        attn_tiles = [keep.tile([P, RES], BF16, name="attn%d" % i) for i in range(TOKEN_TILES)]
        src_tiles = [keep.tile([P, D], BF16, name="src%d" % i) for i in range(TOKEN_TILES)]
        w_raw = [keep.tile([P, PACK, D], BF16, name="w_raw%d" % g) for g in range(PASSES)]

        def load_tokens(i):
            rows = slice(i * P, (i + 1) * P)
            nc.sync.dma_start(out=src_tiles[i][:], in_=src_rows[rows, :])
            nc.sync.dma_start(out=u_tiles[i][:], in_=u_rows[rows, :])
            nc.sync.dma_start(out=attn_tiles[i][:], in_=attn_rows[rows, :])

        def load_weights(g):
            nc.sync.dma_start(
                out=w_raw[g][:].rearrange("p (h e) c -> p h e c", e=2),
                in_=w_out[g * K_PASS : (g + 1) * K_PASS, :].rearrange("(h p e) c -> p h e c", h=2, e=2),
            )

        for n, g in enumerate(PASS_ORDER):
            load_weights(g)
            if n < EARLY_TILES:
                load_tokens(n)
        for i in range(EARLY_TILES, TOKEN_TILES):
            load_tokens(i)

        eps = keep.tile([P, 1], F32)
        nc.vector.memset(eps[:], EPS)
        warm = keep.tile([P, 1], F32)
        nc.scalar.activation(out=warm[:], in_=eps[:], func=ACT.Abs_reciprocal_sqrt)
        ident_bf16 = keep.tile([P, P], BF16)
        make_identity(nc, ident_bf16[:])
        ident_f32 = keep.tile([P, P], F32)
        make_identity(nc, ident_f32[:])
        ones = keep.tile([P, P], BF16)
        nc.vector.memset(ones[:], 1.0)

        vec_cols_ps = psum.tile([P, P], BF16, tag="bank")
        nc.tensor.transpose(vec_cols_ps[:], vec_rows[:], ident_bf16[:])
        vec_cols = keep.tile([P, P], BF16)
        nc.scalar.copy(out=vec_cols[:], in_=vec_cols_ps[:])
        bias_all = keep.tile([P, D], BF16)
        gain_all = keep.tile([P, D], BF16)
        for first_row, spread in ((0, bias_all), (8, gain_all)):
            spread_ps = psum.tile([P, D], BF16, tag="bank")
            for r in range(D // P):
                column = vec_cols[:, first_row + r : first_row + r + 1]
                nc.tensor.transpose(
                    spread_ps[:, r * P : (r + 1) * P], column.to_broadcast([P, P]), ident_bf16[:]
                )
            nc.scalar.copy(out=spread[:], in_=spread_ps[:])

        cat_codes = keep.tile([P, TOKEN_TILES, PASSES * P], U32, align_bytes=64)
        cat_scales = keep.tile([P, TOKEN_TILES, PASSES * P], U8, align_bytes=64)
        w_codes = keep.tile([P, PASSES, D], U32, align_bytes=64)
        w_scales = keep.tile([P, PASSES, D], U8, align_bytes=64)

        ready_tiles = []
        ready_weights = []
        accs = {}
        issued = {}

        def multiply(i, g, h):
            cols = slice(h * BANK, (h + 1) * BANK)
            nc.tensor.matmul_mx(
                out=accs[i][h][:],
                lhsT=cat_codes[:, i, g * P : (g + 1) * P].bitcast(FP8X4),
                lhsT_scale=cat_scales[:, i, g * P : (g + 1) * P],
                rhs=w_codes[:, g, cols].bitcast(FP8X4),
                rhs_scale=w_scales[:, g, cols],
                start=(issued[(i, h)] == 0),
                stop=(issued[(i, h)] == PASSES - 1),
            )
            issued[(i, h)] = issued[(i, h)] + 1

        def flip_two_passes(rows):
            words = rows.bitcast(F32)
            flipped = psum.tile([P, 4, P], F32, tag="bank")
            for q in range(4):
                nc.tensor.transpose(flipped[:, q, :], words[:, q * P : (q + 1) * P], ident_f32[:])
            grouped = stage.tile([P, 2 * K_PASS], BF16, align_bytes=64, name="cat_grouped", bufs=6)
            nc.scalar.copy(
                out=grouped[:].bitcast(F32).rearrange("p (g t h) -> p g t h", t=P, h=2),
                in_=flipped[:].rearrange("p (g h) t -> p g t h", h=2),
            )
            return grouped

        def flip_tokens(i):
            flips = [(RES_PASSES, flip_two_passes(src_tiles[i][:]))]
            for first_pass in range(0, RES_PASSES, 2):
                cols = slice(first_pass * K_PASS, (first_pass + 2) * K_PASS)
                residual = stage.tile([P, 2 * K_PASS], BF16, bufs=4)
                nc.vector.tensor_tensor(
                    out=residual[:], in0=u_tiles[i][:, cols], in1=attn_tiles[i][:, cols], op=ALU.add
                )
                flips.append((first_pass, flip_two_passes(residual[:])))
            return flips

        def quantise_tokens(i, flips):
            for first_pass, grouped in flips:
                cols = slice(first_pass * P, (first_pass + 2) * P)
                nc.vector.quantize_mx(
                    out=cat_codes[:, i, cols].bitcast(FP8X4), scales=cat_scales[:, i, cols], in_=grouped[:]
                )
            accs[i] = [psum.tile([P, BANK], F32, tag="bank", name="acc%d%d" % (i, h)) for h in range(HALVES)]
            for h in range(HALVES):
                issued[(i, h)] = 0
            for g, h in ready_weights:
                multiply(i, g, h)
            ready_tiles.append(i)

        def regroup_weights(g):
            halves = []
            for h in range(HALVES):
                grouped = stage.tile([P, BANK * PACK], BF16, align_bytes=64, name="w_grouped%d" % h)
                copy = nc.vector.tensor_copy if h == 0 else nc.scalar.copy
                copy(
                    out=grouped[:].rearrange("p (c i t) -> p c t i", i=4, t=PACK),
                    in_=w_raw[g][:, :, h * BANK : (h + 1) * BANK].rearrange("p t (c i) -> p c t i", i=4),
                )
                halves.append(grouped)
            return halves

        def quantise_weights(g, h, grouped):
            cols = slice(h * BANK, (h + 1) * BANK)
            nc.vector.quantize_mx(
                out=w_codes[:, g, cols].bitcast(FP8X4), scales=w_scales[:, g, cols], in_=grouped[:]
            )
            for i in ready_tiles:
                multiply(i, g, h)
            ready_weights.append((g, h))

        def centre_and_gain(i):
            z = stage.tile([P, D], F32)
            z_sum = small.tile([P, HALVES], F32)
            for h in range(HALVES):
                cols = slice(h * BANK, (h + 1) * BANK)
                nc.vector.scalar_tensor_tensor(
                    out=z[:, cols],
                    in0=accs[i][h][:],
                    scalar=1.0,
                    in1=bias_all[:, cols],
                    op0=ALU.mult,
                    op1=ALU.add,
                    accum_out=z_sum[:, h : h + 1],
                )
            neg_mean = small.tile([P, 1], F32)
            nc.vector.tensor_scalar(
                out=neg_mean[:],
                in0=z_sum[:, 0:1],
                scalar1=z_sum[:, 1:2],
                scalar2=-1.0 / D,
                op0=ALU.add,
                op1=ALU.mult,
            )
            shifted = []
            for h in range(HALVES):
                cols = slice(h * BANK, (h + 1) * BANK)
                shifted_ps = psum.tile([P, BANK], F32, tag="bank", name="shifted%d" % h)
                nc.tensor.matmul(
                    out=shifted_ps[:], lhsT=ident_bf16[:], rhs=src_tiles[i][:, cols], start=True, stop=False
                )
                nc.tensor.matmul(
                    out=shifted_ps[:], lhsT=ones[:], rhs=shift_row[:, cols], start=False, stop=True
                )
                shifted.append(shifted_ps)

            gained = stage.tile([P, D], F32, bufs=LAG + 1)
            nc.vector.scalar_tensor_tensor(
                out=gained[:], in0=z[:], scalar=neg_mean[:], in1=gain_all[:], op0=ALU.add, op1=ALU.mult
            )

            squares = stage.tile([P, D], BF16)
            sq_sum = small.tile([P, 1], F32)
            nc.scalar.activation(
                out=squares[:], in_=z[:], func=ACT.Square, bias=neg_mean[:], accum_out=sq_sum[:]
            )
            rstd = small.tile([P, 1], F32)
            nc.scalar.activation(
                out=rstd[:], in_=sq_sum[:], func=ACT.Abs_reciprocal_sqrt, bias=eps[:], scale=1.0 / D
            )
            return gained, rstd, shifted

        def scale_and_store(i, gained, rstd, shifted):
            result = stage.tile([P, D], F32)
            for h in range(HALVES):
                cols = slice(h * BANK, (h + 1) * BANK)
                nc.vector.scalar_tensor_tensor(
                    out=result[:, cols],
                    in0=gained[:, cols],
                    scalar=rstd[:],
                    in1=shifted[h][:],
                    op0=ALU.mult,
                    op1=ALU.add,
                )
                nc.sync.dma_start(out=out_rows[i * P : (i + 1) * P, cols], in_=result[:, cols])

        flips = {}
        waiting = None
        for n, g in enumerate(PASS_ORDER):
            halves = regroup_weights(g)
            if waiting is not None:
                quantise_weights(waiting[0], 1, waiting[1])
            quantise_weights(g, 0, halves[0])
            waiting = (g, halves[1])
            if 0 <= n - 1 < EARLY_TILES:
                quantise_tokens(n - 1, flips[n - 1])
            if n < EARLY_TILES:
                flips[n] = flip_tokens(n)
        quantise_weights(waiting[0], 1, waiting[1])

        ends = {}
        for i in range(TOKEN_TILES):
            late = i + EARLY_TILES
            if late < TOKEN_TILES:
                flips[late] = flip_tokens(late)
            if EARLY_TILES <= late - 1 < TOKEN_TILES:
                quantise_tokens(late - 1, flips[late - 1])
            if i >= LAG:
                scale_and_store(i - LAG, *ends[i - LAG])
            ends[i] = centre_and_gain(i)
        for i in range(TOKEN_TILES - LAG, TOKEN_TILES):
            scale_and_store(i, *ends[i])
